import numpy as np
import ml_dtypes

BF16 = ml_dtypes.bfloat16


def bf(x):
    return np.asarray(x, np.float32).astype(BF16)


def f32(x):
    return np.asarray(x, np.float32)


def f64(x):
    return np.asarray(x).astype(np.float64)


def striped(idx):
    return np.tile(idx.reshape(-1, 16).T, (8, 1))


C, S, N, H, DK = 512, 4096, 1024, 4, 128
BASE, EPS_LN, EPS_SM = 10000.0, 1e-5, 1e-9


def pos_encoding():
    div = f32(BASE ** (2.0 * np.arange(C // 2, dtype=np.float64) / C))
    ang = np.arange(N, dtype=np.float32)[None, :] / div[:, None]
    return f32(np.stack([np.sin(f64(ang)), np.cos(f64(ang))], axis=1).reshape(C, N))


def setup_inputs():
    return {
        "emb": f32(np.random.standard_normal((C, S))),
        "pe": pos_encoding(),
        "wq": bf(np.random.standard_normal((C, C)) / np.sqrt(C)),
        "wk": bf(np.random.standard_normal((C, C)) / np.sqrt(C)),
        "wv": bf(np.random.standard_normal((C, C)) / np.sqrt(C)),
        "wo": bf(np.random.standard_normal((C, C)) / np.sqrt(C)),
        "ln_s": f32(1.0 + 0.1 * np.random.standard_normal((C, 1))),
        "ln_b": f32(0.1 * np.random.standard_normal((C, 1))),
        "offs": striped(np.random.permutation(np.tile(np.arange(S), 2))[:N]),
    }


def reference(emb, pe, wq, wk, wv, wo, ln_s, ln_b, offs):
    idx = offs[:16].T.reshape(-1)
    h = f64(emb)[:, idx] + f64(pe)
    q = (f64(wq).T @ h).reshape(H, DK, N)
    k = (f64(wk).T @ h).reshape(H, DK, N)
    v = (f64(wv).T @ h).reshape(H, DK, N)
    sc = np.einsum("adt,adu->atu", q, k) / np.sqrt(DK)
    keep = (np.arange(N)[None, :] < np.arange(N)[:, None])[None]
    mx = np.maximum(np.max(np.where(keep, sc, -np.inf), axis=-1, keepdims=True), 0.0)
    e = np.where(keep, np.exp(sc - mx), 0.0)
    attn = e / (np.sum(e, axis=-1, keepdims=True) + EPS_SM)
    o = np.einsum("atu,adu->adt", attn, v).reshape(C, N)
    r = h + f64(wo).T @ o
    mu = np.mean(r, axis=0, keepdims=True)
    var = np.mean((r - mu) ** 2, axis=0, keepdims=True)
    return (r - mu) / np.sqrt(var + EPS_LN) * f64(ln_s) + f64(ln_b)

@@ -1,0 +1,267 @@
+import math
+
+import concourse.mybir as mybir
+from concourse.masks import make_identity
+
+F32 = mybir.dt.float32
+BF16 = mybir.dt.bfloat16
+U16 = mybir.dt.uint16
+I32 = mybir.dt.int32
+ALU = mybir.AluOpType
+FUNC = mybir.ActivationFunctionType
+
+P = 128
+C = 512
+S = 4096
+N = 1024
+H = 4
+DK = 128
+CB = C // P
+TB = N // P
+BANK = 512
+SCALE = 1.0 / math.sqrt(DK)
+EPS_SM = 1e-9
+EPS_LN = 1e-5
+MASKED = -1e30
+
+FLOPS = 2 * C * C * N * 4 + 2 * 2 * H * DK * (N * (N - 1) // 2)
+
+
+def tile_lumiere1m_b_kernel(tc, emb, pe, wq, wk, wv, wo, ln_s, ln_b, offs, out):
+    nc = tc.nc
+    emb_blocks = emb.rearrange("(b p) s -> b p s", p=P)
+    pe_blocks = pe.rearrange("(b p) n -> b p n", p=P)
+    out_blocks = out.rearrange("(b p) n -> p b n", p=P)
+
+    with (
+        tc.tile_pool(name="const", bufs=1) as const,
+        tc.tile_pool(name="keep", bufs=1) as keep,
+    ):
+        offsets = const.tile([P, N // 16], U16, name="offsets")
+        nc.sync.dma_start(offsets[:], offs)
+
+        ident_f32 = const.tile([P, P], F32, name="ident_f32")
+        make_identity(nc, ident_f32[:])
+        ident_bf = const.tile([P, P], BF16, name="ident_bf")
+        make_identity(nc, ident_bf[:])
+        ahead = const.tile([P, P], I32, name="ahead")
+        nc.gpsimd.iota(ahead[:], pattern=[[1, P]], base=0, channel_multiplier=-1)
+        causal = const.tile([P, P], BF16, name="causal")
+        nc.vector.tensor_scalar(
+            out=causal[:], in0=ahead[:], scalar1=0.0, scalar2=MASKED, op0=ALU.is_ge, op1=ALU.mult
+        )
+        neg_half = const.tile([P, 1], F32, name="neg_half")
+        nc.gpsimd.memset(neg_half[:], -0.5)
+
+        h_t = keep.tile([P, TB, C], F32, name="h_t")
+        q_bf = keep.tile([P, H, N], BF16, name="q_bf")
+        k_bf = keep.tile([P, H, N], BF16, name="k_bf")
+        v_t = keep.tile([P, TB, C], BF16, name="v_t")
+        wo_sb = keep.tile([P, H, C], BF16, name="wo_sb")
+        ln_cols = keep.tile([P, 2 * CB], F32, name="ln_cols")
+
+        with (
+            tc.tile_pool(name="front", bufs=1) as front,
+            tc.psum_pool(name="front_ps", bufs=4) as front_ps,
+        ):
+            table = [front.tile([P, S], F32, name=f"table{b}") for b in range(CB)]
+            pe_sb = [front.tile([P, N], F32, name=f"pe_sb{b}") for b in range(CB)]
+            w_sb = {
+                name: front.tile([P, CB, C], BF16, name=f"w{name}_sb") for name in ("q", "k", "v")
+            }
+            ln_rows = front.tile([P, P], F32, name="ln_rows")
+            nc.gpsimd.memset(ln_rows[:], 0.0)
+
+            for b in range(CB):
+                nc.sync.dma_start(table[b][:], emb_blocks[b])
+                nc.sync.dma_start(pe_sb[b][:], pe_blocks[b])
+            for name, w in (("q", wq), ("k", wk), ("v", wv)):
+                nc.sync.dma_start(w_sb[name][:], w.rearrange("(b p) m -> p b m", p=P))
+            nc.sync.dma_start(wo_sb[:], wo.rearrange("(a p) c -> p a c", p=P))
+            nc.sync.dma_start(ln_rows[0:CB, :], ln_s.rearrange("(b p) o -> b (p o)", p=P))
+            nc.sync.dma_start(ln_rows[CB : 2 * CB, :], ln_b.rearrange("(b p) o -> b (p o)", p=P))
+
+            h = [front.tile([P, N], F32, name=f"h{b}") for b in range(CB)]
+            h_bf = [front.tile([P, N], BF16, name=f"h_bf{b}") for b in range(CB)]
+            for b in range(CB):
+                nc.vector.tensor_tensor(
+                    h[b][:], table[b][:].indirect(offsets[:]), pe_sb[b][:], ALU.add
+                )
+                nc.gpsimd.tensor_copy(h_bf[b][:], h[b][:])
+                for t0 in range(0, TB, 4):
+                    h_flip = front_ps.tile([P, 4, P], F32, name="h_flip", tag="acc")
+                    for i in range(4):
+                        nc.tensor.transpose(
+                            h_flip[:, i, :], h[b][:, (t0 + i) * P : (t0 + i + 1) * P], ident_f32[:]
+                        )
+                    nc.scalar.copy(h_t[:, t0 : t0 + 4, b * P : (b + 1) * P], h_flip[:])
+
+            ln_ps = front_ps.tile([P, P], F32, name="ln_ps", tag="acc")
+            nc.tensor.transpose(ln_ps[:], ln_rows[:], ident_f32[:])
+            nc.vector.tensor_copy(ln_cols[:], ln_ps[:, 0 : 2 * CB])
+
+            for name, dest in (("q", q_bf), ("k", k_bf)):
+                for a in range(H):
+                    for half in range(N // BANK):
+                        acc = front_ps.tile([P, BANK], F32, name="acc", tag="acc")
+                        for b in range(CB):
+                            nc.tensor.matmul(
+                                acc[:],
+                                lhsT=w_sb[name][:, b, a * DK : (a + 1) * DK],
+                                rhs=h_bf[b][:, half * BANK : (half + 1) * BANK],
+                                start=(b == 0),
+                                stop=(b == CB - 1),
+                            )
+                        dest_half = dest[:, a, half * BANK : (half + 1) * BANK]
+                        if half % 2 == 0:
+                            nc.vector.tensor_copy(dest_half, acc[:])
+                        else:
+                            nc.scalar.copy(dest_half, acc[:])
+            for t in range(TB):
+                acc = front_ps.tile([P, BANK], F32, name="acc", tag="acc")
+                for b in range(CB):
+                    nc.tensor.matmul(
+                        acc[:],
+                        lhsT=h_bf[b][:, t * P : (t + 1) * P],
+                        rhs=w_sb["v"][:, b, :],
+                        start=(b == 0),
+                        stop=(b == CB - 1),
+                    )
+                if t % 2 == 0:
+                    nc.vector.tensor_copy(v_t[:, t, :], acc[:])
+                else:
+                    nc.scalar.copy(v_t[:, t, :], acc[:])
+
+        with (
+            tc.tile_pool(name="soft", bufs=3) as soft,
+            tc.tile_pool(name="heads", bufs=2 * H) as heads,
+            tc.tile_pool(name="small", bufs=4) as small,
+            tc.tile_pool(name="tail", bufs=2) as tail,
+            tc.psum_pool(name="sc_ps", bufs=3) as sc_pool,
+            tc.psum_pool(name="tp_ps", bufs=2) as tp_pool,
+            tc.psum_pool(name="one_ps", bufs=1) as one_pool,
+        ):
+            for t in range(TB):
+                seen = (t + 1) * P
+                neg_max = small.tile([P, H, 2], F32, name="neg_max")
+                total = small.tile([P, H], F32, name="total")
+                weights = []
+                for a in range(H):
+                    neg_sc = soft.tile([P, N], F32, name="neg_sc")
+                    pieces = range(0, seen, BANK)
+                    for i, u0 in enumerate(pieces):
+                        width = min(BANK, seen - u0)
+                        sc = sc_pool.tile([P, BANK], F32, name="sc")
+                        last = u0 + width == seen
+                        nc.tensor.matmul(
+                            sc[:, :width],
+                            lhsT=q_bf[:, a, t * P : (t + 1) * P],
+                            rhs=k_bf[:, a, u0 : u0 + width],
+                            start=True,
+                            stop=not last,
+                        )
+                        if last:
+                            nc.tensor.matmul(
+                                sc[:, width - P : width],
+                                lhsT=ident_bf[:],
+                                rhs=causal[:],
+                                start=False,
+                                stop=True,
+                            )
+                        nc.vector.tensor_scalar(
+                            out=neg_sc[:, u0 : u0 + width],
+                            in0=sc[:, :width],
+                            scalar1=-SCALE,
+                            scalar2=0.0 if i == 0 else neg_max[:, a, i - 1 : i],
+                            op0=ALU.mult,
+                            op1=ALU.min,
+                            accum_out=neg_max[:, a, i : i + 1],
+                        )
+                    e = heads.tile([P, N], F32, name="e")
+                    nc.scalar.activation(
+                        out=e[:, :seen],
+                        in_=neg_sc[:, :seen],
+                        func=FUNC.Exp,
+                        bias=neg_max[:, a, len(pieces) - 1 : len(pieces)],
+                        scale=-1.0,
+                        accum_out=total[:, a : a + 1],
+                    )
+                    weights.append(e)
+
+                inv_total = small.tile([P, H], F32, name="inv_total")
+                nc.vector.tensor_scalar(
+                    out=inv_total[:], in0=total[:], scalar1=EPS_SM, scalar2=None, op0=ALU.add
+                )
+                nc.vector.reciprocal(inv_total[:], inv_total[:])
+
+                o_ps = one_pool.tile([P, H, P], F32, name="o_ps")
+                for a in range(H):
+                    attn = soft.tile([P, N], BF16, name="attn")
+                    nc.gpsimd.tensor_scalar(
+                        out=attn[:, :seen],
+                        in0=weights[a][:, :seen],
+                        scalar1=inv_total[:, a : a + 1],
+                        scalar2=1.0,
+                        op0=ALU.mult,
+                        op1=ALU.mult,
+                    )
+                    attn_flip = tp_pool.tile([P, N], BF16, name="attn_flip")
+                    for u in range(t + 1):
+                        nc.tensor.transpose(
+                            attn_flip[:, u * P : (u + 1) * P], attn[:, u * P : (u + 1) * P], ident_bf[:]
+                        )
+                    attn_t = soft.tile([P, N], BF16, name="attn_t")
+                    if a % 2 == 0:
+                        nc.vector.tensor_copy(attn_t[:, :seen], attn_flip[:, :seen])
+                    else:
+                        nc.scalar.copy(attn_t[:, :seen], attn_flip[:, :seen])
+                    for u in range(t + 1):
+                        nc.tensor.matmul(
+                            o_ps[:, a, :],
+                            lhsT=v_t[:, u, a * DK : (a + 1) * DK],
+                            rhs=attn_t[:, u * P : (u + 1) * P],
+                            start=(u == 0),
+                            stop=(u == t),
+                        )
+                o_bf = tail.tile([P, H, P], BF16, name="o_bf")
+                nc.scalar.copy(o_bf[:], o_ps[:])
+
+                r_ps = one_pool.tile([P, C], F32, name="r_ps")
+                for a in range(H):
+                    nc.tensor.matmul(
+                        r_ps[:], lhsT=o_bf[:, a, :], rhs=wo_sb[:, a, :], start=(a == 0), stop=(a == H - 1)
+                    )
+                r_t = tail.tile([P, C], F32, name="r_t")
+                nc.vector.tensor_tensor(r_t[:], r_ps[:], h_t[:, t, :], ALU.add)
+                stats = small.tile([P, 6], F32, name="stats")
+                nc.vector.bn_stats(stats[:], r_t[:])
+                mean_var = small.tile([P, 2], F32, name="mean_var")
+                nc.vector.bn_aggr(mean_var[:], stats[:])
+                var_eps = small.tile([P, 1], F32, name="var_eps")
+                nc.gpsimd.tensor_scalar(
+                    out=var_eps[:], in0=mean_var[:, 1:2], scalar1=1.0, scalar2=EPS_LN, op0=ALU.mult, op1=ALU.add
+                )
+                inv_std = small.tile([P, 1], F32, name="inv_std")
+                nc.gpsimd.tensor_tensor(inv_std[:], var_eps[:], neg_half[:], ALU.pow)
+                y_t = tail.tile([P, C], F32, name="y_t")
+                nc.vector.tensor_scalar(
+                    out=y_t[:],
+                    in0=r_t[:],
+                    scalar1=mean_var[:, 0:1],
+                    scalar2=inv_std[:],
+                    op0=ALU.subtract,
+                    op1=ALU.mult,
+                )
+                y_ps = one_pool.tile([P, CB, P], F32, name="y_ps")
+                for b in range(CB):
+                    nc.tensor.transpose(y_ps[:, b, :], y_t[:, b * P : (b + 1) * P], ident_f32[:])
+                out_sb = tail.tile([P, CB, P], F32, name="out_sb")
+                for b in range(CB):
+                    nc.scalar.activation(
+                        out=out_sb[:, b, :],
+                        in_=y_ps[:, b, :],
+                        func=FUNC.Identity,
+                        bias=ln_cols[:, CB + b : CB + b + 1],
+                        scale=ln_cols[:, b : b + 1],
+                    )
+                nc.sync.dma_start(out_blocks[:, :, t * P : (t + 1) * P], out_sb[:])

@@ -23,6 +23,9 @@ SCALE = 1.0 / math.sqrt(DK)
 EPS_SM = 1e-9
 EPS_LN = 1e-5
 MASKED = -1e30
+EARLY = (0, 1)
+LATE = (2, 3)
+BLOCKS = tuple(reversed(range(TB)))
 
 FLOPS = 2 * C * C * N * 4 + 2 * 2 * H * DK * (N * (N - 1) // 2)
 
@@ -36,6 +39,8 @@ def tile_lumiere1m_b_kernel(tc, emb, pe, wq, wk, wv, wo, ln_s, ln_b, offs, out):
     with (
         tc.tile_pool(name="const", bufs=1) as const,
         tc.tile_pool(name="keep", bufs=1) as keep,
+        tc.psum_pool(name="bank_ps", bufs=3) as bank_pool,
+        tc.psum_pool(name="flip_ps", bufs=2) as flip_pool,
     ):
         offsets = const.tile([P, N // 16], U16, name="offsets")
         nc.sync.dma_start(offsets[:], offs)
@@ -57,175 +62,188 @@ def tile_lumiere1m_b_kernel(tc, emb, pe, wq, wk, wv, wo, ln_s, ln_b, offs, out):
         q_bf = keep.tile([P, H, N], BF16, name="q_bf")
         k_bf = keep.tile([P, H, N], BF16, name="k_bf")
         v_t = keep.tile([P, TB, C], BF16, name="v_t")
+        projected = {"q": q_bf, "k": k_bf, "v": v_t}
+        partial = {
+            "q": keep.tile([P, H, N], F32, name="q_part"),
+            "k": keep.tile([P, H, N], F32, name="k_part"),
+            "v": keep.tile([P, TB, C], F32, name="v_part"),
+        }
+        w_sb = {name: keep.tile([P, CB, C], BF16, name=f"w{name}_sb") for name in ("q", "k", "v")}
         wo_sb = keep.tile([P, H, C], BF16, name="wo_sb")
+        ln_rows = keep.tile([P, P], F32, name="ln_rows")
         ln_cols = keep.tile([P, 2 * CB], F32, name="ln_cols")
+        h = [keep.tile([P, N], F32, name=f"h{b}") for b in range(CB)]
+        h_bf = [keep.tile([P, N], BF16, name=f"h_bf{b}") for b in range(CB)]
+        nc.gpsimd.memset(ln_rows[:], 0.0)
 
         with (
-            tc.tile_pool(name="front", bufs=1) as front,
-            tc.psum_pool(name="front_ps", bufs=4) as front_ps,
+            tc.tile_pool(name="table", bufs=1) as table_pool,
+            tc.psum_pool(name="front_ps", bufs=3) as front_pool,
         ):
-            table = [front.tile([P, S], F32, name=f"table{b}") for b in range(CB)]
-            pe_sb = [front.tile([P, N], F32, name=f"pe_sb{b}") for b in range(CB)]
-            w_sb = {
-                name: front.tile([P, CB, C], BF16, name=f"w{name}_sb") for name in ("q", "k", "v")
-            }
-            ln_rows = front.tile([P, P], F32, name="ln_rows")
-            nc.gpsimd.memset(ln_rows[:], 0.0)
-
-            for b in range(CB):
+            table = [table_pool.tile([P, S], F32, name=f"table{b}") for b in range(CB)]
+            pe_sb = [table_pool.tile([P, N], F32, name=f"pe_sb{b}") for b in range(CB)]
+            for b in EARLY:
                 nc.sync.dma_start(table[b][:], emb_blocks[b])
                 nc.sync.dma_start(pe_sb[b][:], pe_blocks[b])
             for name, w in (("q", wq), ("k", wk), ("v", wv)):
                 nc.sync.dma_start(w_sb[name][:], w.rearrange("(b p) m -> p b m", p=P))
+            for b in LATE:
+                nc.sync.dma_start(table[b][:], emb_blocks[b])
+                nc.sync.dma_start(pe_sb[b][:], pe_blocks[b])
             nc.sync.dma_start(wo_sb[:], wo.rearrange("(a p) c -> p a c", p=P))
             nc.sync.dma_start(ln_rows[0:CB, :], ln_s.rearrange("(b p) o -> b (p o)", p=P))
             nc.sync.dma_start(ln_rows[CB : 2 * CB, :], ln_b.rearrange("(b p) o -> b (p o)", p=P))
 
-            h = [front.tile([P, N], F32, name=f"h{b}") for b in range(CB)]
-            h_bf = [front.tile([P, N], BF16, name=f"h_bf{b}") for b in range(CB)]
-            for b in range(CB):
+            def look_up(b):
                 nc.vector.tensor_tensor(
                     h[b][:], table[b][:].indirect(offsets[:]), pe_sb[b][:], ALU.add
                 )
                 nc.gpsimd.tensor_copy(h_bf[b][:], h[b][:])
+
+            def transpose_h(b):
                 for t0 in range(0, TB, 4):
-                    h_flip = front_ps.tile([P, 4, P], F32, name="h_flip", tag="acc")
+                    h_flip = flip_pool.tile([P, 4, P], F32, name="h_flip", tag="flip")
                     for i in range(4):
                         nc.tensor.transpose(
                             h_flip[:, i, :], h[b][:, (t0 + i) * P : (t0 + i + 1) * P], ident_f32[:]
                         )
                     nc.scalar.copy(h_t[:, t0 : t0 + 4, b * P : (b + 1) * P], h_flip[:])
 
-            ln_ps = front_ps.tile([P, P], F32, name="ln_ps", tag="acc")
-            nc.tensor.transpose(ln_ps[:], ln_rows[:], ident_f32[:])
-            nc.vector.tensor_copy(ln_cols[:], ln_ps[:, 0 : 2 * CB])
-
-            for name, dest in (("q", q_bf), ("k", k_bf)):
-                for a in range(H):
-                    for half in range(N // BANK):
-                        acc = front_ps.tile([P, BANK], F32, name="acc", tag="acc")
-                        for b in range(CB):
+            def project(blocks):
+                for name in ("q", "k", "v"):
+                    for i in range(2 * H):
+                        acc_pool = bank_pool if i % 2 == 0 else front_pool
+                        acc = acc_pool.tile([P, BANK], F32, name="acc", tag="bank")
+                        for b in blocks:
+                            if name == "v":
+                                lhs_t, rhs = h_bf[b][:, i * P : (i + 1) * P], w_sb["v"][:, b, :]
+                            else:
+                                a, half = i // 2, i % 2
+                                lhs_t = w_sb[name][:, b, a * DK : (a + 1) * DK]
+                                rhs = h_bf[b][:, half * BANK : (half + 1) * BANK]
                             nc.tensor.matmul(
-                                acc[:],
-                                lhsT=w_sb[name][:, b, a * DK : (a + 1) * DK],
-                                rhs=h_bf[b][:, half * BANK : (half + 1) * BANK],
-                                start=(b == 0),
-                                stop=(b == CB - 1),
+                                acc[:], lhsT=lhs_t, rhs=rhs, start=(b == blocks[0]), stop=(b == blocks[-1])
                             )
-                        dest_half = dest[:, a, half * BANK : (half + 1) * BANK]
-                        if half % 2 == 0:
-                            nc.vector.tensor_copy(dest_half, acc[:])
+                        if name == "v":
+                            where = (slice(None), i, slice(None))
                         else:
-                            nc.scalar.copy(dest_half, acc[:])
-            for t in range(TB):
-                acc = front_ps.tile([P, BANK], F32, name="acc", tag="acc")
-                for b in range(CB):
-                    nc.tensor.matmul(
-                        acc[:],
-                        lhsT=h_bf[b][:, t * P : (t + 1) * P],
-                        rhs=w_sb["v"][:, b, :],
-                        start=(b == 0),
-                        stop=(b == CB - 1),
-                    )
-                if t % 2 == 0:
-                    nc.vector.tensor_copy(v_t[:, t, :], acc[:])
-                else:
-                    nc.scalar.copy(v_t[:, t, :], acc[:])
+                            where = (slice(None), i // 2, slice((i % 2) * BANK, (i % 2 + 1) * BANK))
+                        if blocks == LATE:
+                            nc.vector.tensor_tensor(
+                                projected[name][where], acc[:], partial[name][where], ALU.add
+                            )
+                        elif i % 2 == 0:
+                            nc.scalar.copy(partial[name][where], acc[:])
+                        else:
+                            nc.vector.tensor_copy(partial[name][where], acc[:])
+
+            for b in EARLY:
+                look_up(b)
+                transpose_h(b)
+            project(EARLY)
+            for b in LATE:
+                look_up(b)
+            project(LATE)
+            for b in LATE:
+                transpose_h(b)
+
+        ln_ps = bank_pool.tile([P, P], F32, name="ln_ps", tag="bank")
+        nc.tensor.transpose(ln_ps[:], ln_rows[:], ident_f32[:])
+        nc.vector.tensor_copy(ln_cols[:], ln_ps[:, 0 : 2 * CB])
 
         with (
-            tc.tile_pool(name="soft", bufs=3) as soft,
-            tc.tile_pool(name="heads", bufs=2 * H) as heads,
-            tc.tile_pool(name="small", bufs=4) as small,
-            tc.tile_pool(name="tail", bufs=2) as tail,
-            tc.psum_pool(name="sc_ps", bufs=3) as sc_pool,
-            tc.psum_pool(name="tp_ps", bufs=2) as tp_pool,
+            tc.tile_pool(name="rows", bufs=4) as rows_pool,
+            tc.tile_pool(name="attn", bufs=2 * H + 2) as attn_pool,
+            tc.tile_pool(name="turned", bufs=4) as turned_pool,
+            tc.tile_pool(name="small", bufs=8) as small,
+            tc.tile_pool(name="tail", bufs=3) as tail,
             tc.psum_pool(name="one_ps", bufs=1) as one_pool,
         ):
-            for t in range(TB):
-                seen = (t + 1) * P
-                neg_max = small.tile([P, H, 2], F32, name="neg_max")
-                total = small.tile([P, H], F32, name="total")
-                weights = []
-                for a in range(H):
-                    neg_sc = soft.tile([P, N], F32, name="neg_sc")
-                    pieces = range(0, seen, BANK)
-                    for i, u0 in enumerate(pieces):
-                        width = min(BANK, seen - u0)
-                        sc = sc_pool.tile([P, BANK], F32, name="sc")
-                        last = u0 + width == seen
-                        nc.tensor.matmul(
-                            sc[:, :width],
-                            lhsT=q_bf[:, a, t * P : (t + 1) * P],
-                            rhs=k_bf[:, a, u0 : u0 + width],
-                            start=True,
-                            stop=not last,
-                        )
-                        if last:
-                            nc.tensor.matmul(
-                                sc[:, width - P : width],
-                                lhsT=ident_bf[:],
-                                rhs=causal[:],
-                                start=False,
-                                stop=True,
-                            )
-                        nc.vector.tensor_scalar(
-                            out=neg_sc[:, u0 : u0 + width],
-                            in0=sc[:, :width],
-                            scalar1=-SCALE,
-                            scalar2=0.0 if i == 0 else neg_max[:, a, i - 1 : i],
-                            op0=ALU.mult,
-                            op1=ALU.min,
-                            accum_out=neg_max[:, a, i : i + 1],
-                        )
-                    e = heads.tile([P, N], F32, name="e")
-                    nc.scalar.activation(
-                        out=e[:, :seen],
-                        in_=neg_sc[:, :seen],
-                        func=FUNC.Exp,
-                        bias=neg_max[:, a, len(pieces) - 1 : len(pieces)],
-                        scale=-1.0,
-                        accum_out=total[:, a : a + 1],
-                    )
-                    weights.append(e)
 
-                inv_total = small.tile([P, H], F32, name="inv_total")
+            def exp_rows(t, a):
+                seen = (t + 1) * P
+                neg_sc = rows_pool.tile([P, N], F32, name="neg_sc")
+                neg_max = small.tile([P, 2], F32, name="neg_max")
+                pieces = range(0, seen, BANK)
+                for i, u0 in enumerate(pieces):
+                    width = min(BANK, seen - u0)
+                    sc = bank_pool.tile([P, BANK], F32, name="sc", tag="bank")
+                    last = u0 + width == seen
+                    nc.tensor.matmul(
+                        sc[:, :width],
+                        lhsT=q_bf[:, a, t * P : (t + 1) * P],
+                        rhs=k_bf[:, a, u0 : u0 + width],
+                        start=True,
+                        stop=not last,
+                    )
+                    if last:
+                        nc.tensor.matmul(
+                            sc[:, width - P : width], lhsT=ident_bf[:], rhs=causal[:], start=False, stop=True
+                        )
+                    nc.vector.tensor_scalar(
+                        out=neg_sc[:, u0 : u0 + width],
+                        in0=sc[:, :width],
+                        scalar1=-SCALE,
+                        scalar2=0.0 if i == 0 else neg_max[:, i - 1 : i],
+                        op0=ALU.mult,
+                        op1=ALU.min,
+                        accum_out=neg_max[:, i : i + 1],
+                    )
+                e = rows_pool.tile([P, N], F32, name="e")
+                total = small.tile([P, 1], F32, name="total")
+                nc.scalar.activation(
+                    out=e[:, :seen],
+                    in_=neg_sc[:, :seen],
+                    func=FUNC.Exp,
+                    bias=neg_max[:, len(pieces) - 1 : len(pieces)],
+                    scale=-1.0,
+                    accum_out=total[:],
+                )
+                return e, total
+
+            def normalise(t, e, total):
+                seen = (t + 1) * P
+                inv_total = small.tile([P, 1], F32, name="inv_total")
                 nc.vector.tensor_scalar(
                     out=inv_total[:], in0=total[:], scalar1=EPS_SM, scalar2=None, op0=ALU.add
                 )
                 nc.vector.reciprocal(inv_total[:], inv_total[:])
+                attn = attn_pool.tile([P, N], BF16, name="attn")
+                nc.gpsimd.tensor_scalar(
+                    out=attn[:, :seen],
+                    in0=e[:, :seen],
+                    scalar1=inv_total[:],
+                    scalar2=0.0,
+                    op0=ALU.mult,
+                    op1=ALU.add,
+                )
+                return attn
 
-                o_ps = one_pool.tile([P, H, P], F32, name="o_ps")
-                for a in range(H):
-                    attn = soft.tile([P, N], BF16, name="attn")
-                    nc.gpsimd.tensor_scalar(
-                        out=attn[:, :seen],
-                        in0=weights[a][:, :seen],
-                        scalar1=inv_total[:, a : a + 1],
-                        scalar2=1.0,
-                        op0=ALU.mult,
-                        op1=ALU.mult,
+            def turn(t, a, attn):
+                seen = (t + 1) * P
+                attn_flip = flip_pool.tile([P, N], BF16, name="attn_flip", tag="flip")
+                for u in range(t + 1):
+                    nc.tensor.transpose(
+                        attn_flip[:, u * P : (u + 1) * P], attn[:, u * P : (u + 1) * P], ident_bf[:]
                     )
-                    attn_flip = tp_pool.tile([P, N], BF16, name="attn_flip")
-                    for u in range(t + 1):
-                        nc.tensor.transpose(
-                            attn_flip[:, u * P : (u + 1) * P], attn[:, u * P : (u + 1) * P], ident_bf[:]
-                        )
-                    attn_t = soft.tile([P, N], BF16, name="attn_t")
-                    if a % 2 == 0:
-                        nc.vector.tensor_copy(attn_t[:, :seen], attn_flip[:, :seen])
-                    else:
-                        nc.scalar.copy(attn_t[:, :seen], attn_flip[:, :seen])
-                    for u in range(t + 1):
-                        nc.tensor.matmul(
-                            o_ps[:, a, :],
-                            lhsT=v_t[:, u, a * DK : (a + 1) * DK],
-                            rhs=attn_t[:, u * P : (u + 1) * P],
-                            start=(u == 0),
-                            stop=(u == t),
-                        )
-                o_bf = tail.tile([P, H, P], BF16, name="o_bf")
-                nc.scalar.copy(o_bf[:], o_ps[:])
+                attn_t = turned_pool.tile([P, N], BF16, name="attn_t")
+                if a % 2 == 0:
+                    nc.vector.tensor_copy(attn_t[:, :seen], attn_flip[:, :seen])
+                else:
+                    nc.scalar.copy(attn_t[:, :seen], attn_flip[:, :seen])
+                return attn_t
 
+            def weigh(t, a, attn_t, o_ps):
+                for u in range(t + 1):
+                    nc.tensor.matmul(
+                        o_ps[:, a, :],
+                        lhsT=v_t[:, u, a * DK : (a + 1) * DK],
+                        rhs=attn_t[:, u * P : (u + 1) * P],
+                        start=(u == 0),
+                        stop=(u == t),
+                    )
+
+            def finish(t, o_bf):
                 r_ps = one_pool.tile([P, C], F32, name="r_ps")
                 for a in range(H):
                     nc.tensor.matmul(
@@ -265,3 +283,32 @@ def tile_lumiere1m_b_kernel(tc, emb, pe, wq, wk, wv, wo, ln_s, ln_b, offs, out):
                         scale=ln_cols[:, b : b + 1],
                     )
                 nc.sync.dma_start(out_blocks[:, :, t * P : (t + 1) * P], out_sb[:])
+
+            attn_of = {}
+            o_of = {}
+            for step in range(TB + 2):
+                first = BLOCKS[step] if step < TB else None
+                second = BLOCKS[step - 1] if 1 <= step <= TB else None
+                third = BLOCKS[step - 2] if step >= 2 else None
+                if first is not None:
+                    attn_of[first] = []
+                if second is not None:
+                    o_ps = one_pool.tile([P, H, P], F32, name="o_ps")
+                for a in range(H + 1):
+                    if first is not None and a < H:
+                        exps = exp_rows(first, a)
+                    if first is not None and a > 0:
+                        attn_of[first].append(normalise(first, *waiting_exps))
+                    if second is not None and a < H:
+                        turned = turn(second, a, attn_of[second][a])
+                    if second is not None and a > 0:
+                        weigh(second, a - 1, waiting_turned, o_ps)
+                    if first is not None:
+                        waiting_exps = exps
+                    if second is not None:
+                        waiting_turned = turned
+                if second is not None:
+                    o_of[second] = tail.tile([P, H, P], BF16, name="o_bf")
+                    nc.scalar.copy(o_of[second][:], o_ps[:])
+                if third is not None:
+                    finish(third, o_of[third])

@@ -25,7 +25,7 @@ EPS_LN = 1e-5
 MASKED = -1e30
 EARLY = (0, 1)
 LATE = (2, 3)
-BLOCKS = tuple(reversed(range(TB)))
+BLOCKS = tuple(range(TB))
 
 FLOPS = 2 * C * C * N * 4 + 2 * 2 * H * DK * (N * (N - 1) // 2)
 
@@ -39,7 +39,7 @@ def tile_lumiere1m_b_kernel(tc, emb, pe, wq, wk, wv, wo, ln_s, ln_b, offs, out):
     with (
         tc.tile_pool(name="const", bufs=1) as const,
         tc.tile_pool(name="keep", bufs=1) as keep,
-        tc.psum_pool(name="bank_ps", bufs=3) as bank_pool,
+        tc.psum_pool(name="bank_ps", bufs=4) as bank_pool,
         tc.psum_pool(name="flip_ps", bufs=2) as flip_pool,
     ):
         offsets = const.tile([P, N // 16], U16, name="offsets")
@@ -78,7 +78,7 @@ def tile_lumiere1m_b_kernel(tc, emb, pe, wq, wk, wv, wo, ln_s, ln_b, offs, out):
 
         with (
             tc.tile_pool(name="table", bufs=1) as table_pool,
-            tc.psum_pool(name="front_ps", bufs=3) as front_pool,
+            tc.psum_pool(name="front_ps", bufs=2) as front_pool,
         ):
             table = [table_pool.tile([P, S], F32, name=f"table{b}") for b in range(CB)]
             pe_sb = [table_pool.tile([P, N], F32, name=f"pe_sb{b}") for b in range(CB)]
@@ -95,10 +95,13 @@ def tile_lumiere1m_b_kernel(tc, emb, pe, wq, wk, wv, wo, ln_s, ln_b, offs, out):
             nc.sync.dma_start(ln_rows[CB : 2 * CB, :], ln_b.rearrange("(b p) o -> b (p o)", p=P))
 
             def look_up(b):
-                nc.vector.tensor_tensor(
-                    h[b][:], table[b][:].indirect(offsets[:]), pe_sb[b][:], ALU.add
-                )
-                nc.gpsimd.tensor_copy(h_bf[b][:], h[b][:])
+                for half in range(N // BANK):
+                    tokens = slice(half * BANK, (half + 1) * BANK)
+                    piece = offsets[:, half * (BANK // 16) : (half + 1) * (BANK // 16)]
+                    nc.vector.tensor_tensor(
+                        h[b][:, tokens], table[b][:].indirect(piece), pe_sb[b][:, tokens], ALU.add
+                    )
+                    nc.gpsimd.tensor_copy(h_bf[b][:, tokens], h[b][:, tokens])
 
             def transpose_h(b):
                 for t0 in range(0, TB, 4):
@@ -112,7 +115,7 @@ def tile_lumiere1m_b_kernel(tc, emb, pe, wq, wk, wv, wo, ln_s, ln_b, offs, out):
             def project(blocks):
                 for name in ("q", "k", "v"):
                     for i in range(2 * H):
-                        acc_pool = bank_pool if i % 2 == 0 else front_pool
+                        acc_pool = bank_pool if i % 3 < 2 else front_pool
                         acc = acc_pool.tile([P, BANK], F32, name="acc", tag="bank")
                         for b in blocks:
                             if name == "v":
@@ -152,7 +155,7 @@ def tile_lumiere1m_b_kernel(tc, emb, pe, wq, wk, wv, wo, ln_s, ln_b, offs, out):
         nc.vector.tensor_copy(ln_cols[:], ln_ps[:, 0 : 2 * CB])
 
         with (
-            tc.tile_pool(name="rows", bufs=4) as rows_pool,
+            tc.tile_pool(name="rows", bufs=6) as rows_pool,
             tc.tile_pool(name="attn", bufs=2 * H + 2) as attn_pool,
             tc.tile_pool(name="turned", bufs=4) as turned_pool,
             tc.tile_pool(name="small", bufs=8) as small,
@@ -243,8 +246,8 @@ def tile_lumiere1m_b_kernel(tc, emb, pe, wq, wk, wv, wo, ln_s, ln_b, offs, out):
                         stop=(u == t),
                     )
 
-            def finish(t, o_bf):
-                r_ps = one_pool.tile([P, C], F32, name="r_ps")
+            def normalised_residual(t, o_bf):
+                r_ps = one_pool.tile([P, C], F32, name="r_ps", tag="post")
                 for a in range(H):
                     nc.tensor.matmul(
                         r_ps[:], lhsT=o_bf[:, a, :], rhs=wo_sb[:, a, :], start=(a == 0), stop=(a == H - 1)
@@ -270,7 +273,10 @@ def tile_lumiere1m_b_kernel(tc, emb, pe, wq, wk, wv, wo, ln_s, ln_b, offs, out):
                     op0=ALU.subtract,
                     op1=ALU.mult,
                 )
-                y_ps = one_pool.tile([P, CB, P], F32, name="y_ps")
+                return y_t
+
+            def store(t, y_t):
+                y_ps = one_pool.tile([P, CB, P], F32, name="y_ps", tag="post")
                 for b in range(CB):
                     nc.tensor.transpose(y_ps[:, b, :], y_t[:, b * P : (b + 1) * P], ident_f32[:])
                 out_sb = tail.tile([P, CB, P], F32, name="out_sb")
@@ -286,10 +292,12 @@ def tile_lumiere1m_b_kernel(tc, emb, pe, wq, wk, wv, wo, ln_s, ln_b, offs, out):
 
             attn_of = {}
             o_of = {}
-            for step in range(TB + 2):
+            y_of = {}
+            for step in range(TB + 3):
                 first = BLOCKS[step] if step < TB else None
                 second = BLOCKS[step - 1] if 1 <= step <= TB else None
-                third = BLOCKS[step - 2] if step >= 2 else None
+                third = BLOCKS[step - 2] if 2 <= step <= TB + 1 else None
+                fourth = BLOCKS[step - 3] if step >= 3 else None
                 if first is not None:
                     attn_of[first] = []
                 if second is not None:
@@ -311,4 +319,6 @@ def tile_lumiere1m_b_kernel(tc, emb, pe, wq, wk, wv, wo, ln_s, ln_b, offs, out):
                     o_of[second] = tail.tile([P, H, P], BF16, name="o_bf")
                     nc.scalar.copy(o_of[second][:], o_ps[:])
                 if third is not None:
-                    finish(third, o_of[third])
+                    y_of[third] = normalised_residual(third, o_of[third])
+                if fourth is not None:
+                    store(fourth, y_of[fourth])

@@ -25,7 +25,7 @@ EPS_LN = 1e-5
 MASKED = -1e30
 EARLY = (0, 1)
 LATE = (2, 3)
-BLOCKS = tuple(range(TB))
+BLOCKS = tuple(reversed(range(TB)))
 
 FLOPS = 2 * C * C * N * 4 + 2 * 2 * H * DK * (N * (N - 1) // 2)
 

@@ -25,7 +25,7 @@ EPS_LN = 1e-5
 MASKED = -1e30
 EARLY = (0, 1)
 LATE = (2, 3)
-BLOCKS = tuple(reversed(range(TB)))
+BLOCKS = tuple(range(TB))
 
 FLOPS = 2 * C * C * N * 4 + 2 * 2 * H * DK * (N * (N - 1) // 2)
 
@@ -226,8 +226,12 @@ def tile_lumiere1m_b_kernel(tc, emb, pe, wq, wk, wv, wo, ln_s, ln_b, offs, out):
                 seen = (t + 1) * P
                 attn_flip = flip_pool.tile([P, N], BF16, name="attn_flip", tag="flip")
                 for u in range(t + 1):
-                    nc.tensor.transpose(
-                        attn_flip[:, u * P : (u + 1) * P], attn[:, u * P : (u + 1) * P], ident_bf[:]
+                    nc.tensor.matmul(
+                        attn_flip[:, u * P : (u + 1) * P],
+                        lhsT=attn[:, u * P : (u + 1) * P],
+                        rhs=ident_bf[:],
+                        start=True,
+                        stop=True,
                     )
                 attn_t = turned_pool.tile([P, N], BF16, name="attn_t")
                 if a % 2 == 0:

@@ -101,7 +101,7 @@ def tile_lumiere1m_b_kernel(tc, emb, pe, wq, wk, wv, wo, ln_s, ln_b, offs, out):
                     nc.vector.tensor_tensor(
                         h[b][:, tokens], table[b][:].indirect(piece), pe_sb[b][:, tokens], ALU.add
                     )
-                    nc.gpsimd.tensor_copy(h_bf[b][:, tokens], h[b][:, tokens])
+                    nc.scalar.copy(h_bf[b][:, tokens], h[b][:, tokens])
 
             def transpose_h(b):
                 for t0 in range(0, TB, 4):
@@ -202,15 +202,14 @@ def tile_lumiere1m_b_kernel(tc, emb, pe, wq, wk, wv, wo, ln_s, ln_b, offs, out):
                     scale=-1.0,
                     accum_out=total[:],
                 )
-                return e, total
+                padded = small.tile([P, 1], F32, name="padded")
+                nc.scalar.activation(out=padded[:], in_=total[:], func=FUNC.Copy, bias=EPS_SM)
+                return e, padded
 
-            def normalise(t, e, total):
+            def normalise(t, e, padded):
                 seen = (t + 1) * P
                 inv_total = small.tile([P, 1], F32, name="inv_total")
-                nc.vector.tensor_scalar(
-                    out=inv_total[:], in0=total[:], scalar1=EPS_SM, scalar2=None, op0=ALU.add
-                )
-                nc.vector.reciprocal(inv_total[:], inv_total[:])
+                nc.vector.reciprocal(inv_total[:], padded[:])
                 attn = attn_pool.tile([P, N], BF16, name="attn")
                 nc.gpsimd.tensor_scalar(
                     out=attn[:, :seen],
@@ -268,14 +267,13 @@ def tile_lumiere1m_b_kernel(tc, emb, pe, wq, wk, wv, wo, ln_s, ln_b, offs, out):
                 )
                 inv_std = small.tile([P, 1], F32, name="inv_std")
                 nc.gpsimd.tensor_tensor(inv_std[:], var_eps[:], neg_half[:], ALU.pow)
+                shift = small.tile([P, 1], F32, name="shift")
+                nc.gpsimd.tensor_scalar(
+                    out=shift[:], in0=mean_var[:, 0:1], scalar1=inv_std[:], scalar2=-1.0, op0=ALU.mult, op1=ALU.mult
+                )
                 y_t = tail.tile([P, C], F32, name="y_t")
-                nc.vector.tensor_scalar(
-                    out=y_t[:],
-                    in0=r_t[:],
-                    scalar1=mean_var[:, 0:1],
-                    scalar2=inv_std[:],
-                    op0=ALU.subtract,
-                    op1=ALU.mult,
+                nc.gpsimd.tensor_scalar(
+                    out=y_t[:], in0=r_t[:], scalar1=inv_std[:], scalar2=shift[:], op0=ALU.mult, op1=ALU.add
                 )
                 return y_t
 

@@ -82,14 +82,18 @@ def tile_lumiere1m_b_kernel(tc, emb, pe, wq, wk, wv, wo, ln_s, ln_b, offs, out):
         ):
             table = [table_pool.tile([P, S], F32, name=f"table{b}") for b in range(CB)]
             pe_sb = [table_pool.tile([P, N], F32, name=f"pe_sb{b}") for b in range(CB)]
-            for b in EARLY:
-                nc.sync.dma_start(table[b][:], emb_blocks[b])
-                nc.sync.dma_start(pe_sb[b][:], pe_blocks[b])
-            for name, w in (("q", wq), ("k", wk), ("v", wv)):
-                nc.sync.dma_start(w_sb[name][:], w.rearrange("(b p) m -> p b m", p=P))
-            for b in LATE:
-                nc.sync.dma_start(table[b][:], emb_blocks[b])
-                nc.sync.dma_start(pe_sb[b][:], pe_blocks[b])
+            def load_weights(name, w, blocks):
+                rows = w.rearrange("(b p) m -> p b m", p=P)
+                nc.sync.dma_start(w_sb[name][:, blocks[0] : blocks[-1] + 1, :], rows[:, blocks[0] : blocks[-1] + 1, :])
+
+            for blocks in (EARLY, LATE):
+                for b in blocks:
+                    nc.sync.dma_start(table[b][:], emb_blocks[b])
+                    nc.sync.dma_start(pe_sb[b][:], pe_blocks[b])
+                    if b == blocks[0]:
+                        load_weights("q", wq, blocks)
+                load_weights("k", wk, blocks)
+                load_weights("v", wv, blocks)
             nc.sync.dma_start(wo_sb[:], wo.rearrange("(a p) c -> p a c", p=P))
             nc.sync.dma_start(ln_rows[0:CB, :], ln_s.rearrange("(b p) o -> b (p o)", p=P))
             nc.sync.dma_start(ln_rows[CB : 2 * CB, :], ln_b.rearrange("(b p) o -> b (p o)", p=P))
@@ -112,41 +116,43 @@ def tile_lumiere1m_b_kernel(tc, emb, pe, wq, wk, wv, wo, ln_s, ln_b, offs, out):
                         )
                     nc.scalar.copy(h_t[:, t0 : t0 + 4, b * P : (b + 1) * P], h_flip[:])
 
-            def project(blocks):
-                for name in ("q", "k", "v"):
-                    for i in range(2 * H):
-                        acc_pool = bank_pool if i % 3 < 2 else front_pool
-                        acc = acc_pool.tile([P, BANK], F32, name="acc", tag="bank")
-                        for b in blocks:
-                            if name == "v":
-                                lhs_t, rhs = h_bf[b][:, i * P : (i + 1) * P], w_sb["v"][:, b, :]
-                            else:
-                                a, half = i // 2, i % 2
-                                lhs_t = w_sb[name][:, b, a * DK : (a + 1) * DK]
-                                rhs = h_bf[b][:, half * BANK : (half + 1) * BANK]
-                            nc.tensor.matmul(
-                                acc[:], lhsT=lhs_t, rhs=rhs, start=(b == blocks[0]), stop=(b == blocks[-1])
-                            )
+            def project(blocks, banks):
+                for n, (name, i) in enumerate(banks):
+                    acc_pool = bank_pool if n % 3 < 2 else front_pool
+                    acc = acc_pool.tile([P, BANK], F32, name="acc", tag="bank")
+                    for b in blocks:
                         if name == "v":
-                            where = (slice(None), i, slice(None))
+                            lhs_t, rhs = h_bf[b][:, i * P : (i + 1) * P], w_sb["v"][:, b, :]
                         else:
-                            where = (slice(None), i // 2, slice((i % 2) * BANK, (i % 2 + 1) * BANK))
-                        if blocks == LATE:
-                            nc.vector.tensor_tensor(
-                                projected[name][where], acc[:], partial[name][where], ALU.add
-                            )
-                        elif i % 2 == 0:
-                            nc.scalar.copy(partial[name][where], acc[:])
-                        else:
-                            nc.vector.tensor_copy(partial[name][where], acc[:])
+                            a, half = i // 2, i % 2
+                            lhs_t = w_sb[name][:, b, a * DK : (a + 1) * DK]
+                            rhs = h_bf[b][:, half * BANK : (half + 1) * BANK]
+                        nc.tensor.matmul(acc[:], lhsT=lhs_t, rhs=rhs, start=(b == blocks[0]), stop=(b == blocks[-1]))
+                    if name == "v":
+                        where = (slice(None), i, slice(None))
+                    else:
+                        where = (slice(None), i // 2, slice((i % 2) * BANK, (i % 2 + 1) * BANK))
+                    if blocks == LATE:
+                        nc.vector.tensor_tensor(projected[name][where], acc[:], partial[name][where], ALU.add)
+                    elif n % 2 == 0:
+                        nc.scalar.copy(partial[name][where], acc[:])
+                    else:
+                        nc.vector.tensor_copy(partial[name][where], acc[:])
+
+            by_name = [(name, i) for name in ("q", "k", "v") for i in range(2 * H)]
+            by_half = []
+            for half in range(N // BANK):
+                for a in range(H):
+                    by_half.extend([("q", 2 * a + half), ("k", 2 * a + half)])
+                by_half.extend([("v", half * (TB // 2) + i) for i in range(TB // 2)])
 
             for b in EARLY:
                 look_up(b)
                 transpose_h(b)
-            project(EARLY)
+            project(EARLY, by_name)
             for b in LATE:
                 look_up(b)
-            project(LATE)
+            project(LATE, by_half)
             for b in LATE:
                 transpose_h(b)
 

@@ -268,18 +268,14 @@ def tile_lumiere1m_b_kernel(tc, emb, pe, wq, wk, wv, wo, ln_s, ln_b, offs, out):
                 mean_var = small.tile([P, 2], F32, name="mean_var")
                 nc.vector.bn_aggr(mean_var[:], stats[:])
                 var_eps = small.tile([P, 1], F32, name="var_eps")
-                nc.gpsimd.tensor_scalar(
-                    out=var_eps[:], in0=mean_var[:, 1:2], scalar1=1.0, scalar2=EPS_LN, op0=ALU.mult, op1=ALU.add
-                )
+                nc.scalar.activation(out=var_eps[:], in_=mean_var[:, 1:2], func=FUNC.Copy, bias=EPS_LN)
+                neg_mean = small.tile([P, 1], F32, name="neg_mean")
+                nc.scalar.mul(neg_mean[:], mean_var[:, 0:1], -1.0)
                 inv_std = small.tile([P, 1], F32, name="inv_std")
                 nc.gpsimd.tensor_tensor(inv_std[:], var_eps[:], neg_half[:], ALU.pow)
-                shift = small.tile([P, 1], F32, name="shift")
-                nc.gpsimd.tensor_scalar(
-                    out=shift[:], in0=mean_var[:, 0:1], scalar1=inv_std[:], scalar2=-1.0, op0=ALU.mult, op1=ALU.mult
-                )
                 y_t = tail.tile([P, C], F32, name="y_t")
                 nc.gpsimd.tensor_scalar(
-                    out=y_t[:], in0=r_t[:], scalar1=inv_std[:], scalar2=shift[:], op0=ALU.mult, op1=ALU.add
+                    out=y_t[:], in0=r_t[:], scalar1=neg_mean[:], scalar2=inv_std[:], op0=ALU.add, op1=ALU.mult
                 )
                 return y_t
 
@@ -310,6 +306,7 @@ def tile_lumiere1m_b_kernel(tc, emb, pe, wq, wk, wv, wo, ln_s, ln_b, offs, out):
                     attn_of[first] = []
                 if second is not None:
                     o_ps = one_pool.tile([P, H, P], F32, name="o_ps")
+                    o_of[second] = tail.tile([P, H, P], BF16, name="o_bf")
                 for a in range(H + 1):
                     if first is not None and a < H:
                         exps = exp_rows(first, a)
@@ -319,13 +316,11 @@ def tile_lumiere1m_b_kernel(tc, emb, pe, wq, wk, wv, wo, ln_s, ln_b, offs, out):
                         turned = turn(second, a, attn_of[second][a])
                     if second is not None and a > 0:
                         weigh(second, a - 1, waiting_turned, o_ps)
+                        nc.scalar.copy(o_of[second][:, a - 1, :], o_ps[:, a - 1, :])
                     if first is not None:
                         waiting_exps = exps
                     if second is not None:
                         waiting_turned = turned
-                if second is not None:
-                    o_of[second] = tail.tile([P, H, P], BF16, name="o_bf")
-                    nc.scalar.copy(o_of[second][:], o_ps[:])
                 if third is not None:
                     y_of[third] = normalised_residual(third, o_of[third])
                 if fourth is not None:

@@ -25,6 +25,8 @@ EPS_LN = 1e-5
 MASKED = -1e30
 EARLY = (0, 1)
 LATE = (2, 3)
+FIRST = {"q": (0,), "k": (0, 1), "v": (0, 1)}
+REST = {"q": (1, 2, 3), "k": (2, 3), "v": (2, 3)}
 BLOCKS = tuple(range(TB))
 
 FLOPS = 2 * C * C * N * 4 + 2 * 2 * H * DK * (N * (N - 1) // 2)
@@ -116,8 +118,9 @@ def tile_lumiere1m_b_kernel(tc, emb, pe, wq, wk, wv, wo, ln_s, ln_b, offs, out):
                         )
                     nc.scalar.copy(h_t[:, t0 : t0 + 4, b * P : (b + 1) * P], h_flip[:])
 
-            def project(blocks, banks):
+            def project(blocks_of, banks):
                 for n, (name, i) in enumerate(banks):
+                    blocks = blocks_of[name]
                     acc_pool = bank_pool if n % 3 < 2 else front_pool
                     acc = acc_pool.tile([P, BANK], F32, name="acc", tag="bank")
                     for b in blocks:
@@ -132,27 +135,29 @@ def tile_lumiere1m_b_kernel(tc, emb, pe, wq, wk, wv, wo, ln_s, ln_b, offs, out):
                         where = (slice(None), i, slice(None))
                     else:
                         where = (slice(None), i // 2, slice((i % 2) * BANK, (i % 2 + 1) * BANK))
-                    if blocks == LATE:
+                    if blocks_of == REST:
                         nc.vector.tensor_tensor(projected[name][where], acc[:], partial[name][where], ALU.add)
                     elif n % 2 == 0:
                         nc.scalar.copy(partial[name][where], acc[:])
                     else:
                         nc.vector.tensor_copy(partial[name][where], acc[:])
 
-            by_name = [(name, i) for name in ("q", "k", "v") for i in range(2 * H)]
+            by_name = {name: [(name, i) for i in range(2 * H)] for name in ("q", "k", "v")}
             by_half = []
             for half in range(N // BANK):
                 for a in range(H):
                     by_half.extend([("q", 2 * a + half), ("k", 2 * a + half)])
                 by_half.extend([("v", half * (TB // 2) + i) for i in range(TB // 2)])
 
-            for b in EARLY:
-                look_up(b)
-                transpose_h(b)
-            project(EARLY, by_name)
+            look_up(0)
+            transpose_h(0)
+            project(FIRST, by_name["q"])
+            look_up(1)
+            transpose_h(1)
+            project(FIRST, by_name["k"] + by_name["v"])
             for b in LATE:
                 look_up(b)
-            project(LATE, by_half)
+            project(REST, by_half)
             for b in LATE:
                 transpose_h(b)
 

@@ -27,7 +27,14 @@ EARLY = (0, 1)
 LATE = (2, 3)
 FIRST = {"q": (0,), "k": (0, 1), "v": (0, 1)}
 REST = {"q": (1, 2, 3), "k": (2, 3), "v": (2, 3)}
-BLOCKS = tuple(range(TB))
+UNITS = [(t, a) for t in range(TB) for a in range(H)]
+NORMALISE = 1
+TURN = 6
+WEIGH = 8
+RESIDUAL = 9
+CENTRE = 12
+LATE_FROM = 2
+STORE = 15
 
 FLOPS = 2 * C * C * N * 4 + 2 * 2 * H * DK * (N * (N - 1) // 2)
 
@@ -42,7 +49,7 @@ def tile_lumiere1m_b_kernel(tc, emb, pe, wq, wk, wv, wo, ln_s, ln_b, offs, out):
         tc.tile_pool(name="const", bufs=1) as const,
         tc.tile_pool(name="keep", bufs=1) as keep,
         tc.psum_pool(name="bank_ps", bufs=4) as bank_pool,
-        tc.psum_pool(name="flip_ps", bufs=2) as flip_pool,
+        tc.psum_pool(name="flip_ps", bufs=3) as flip_pool,
     ):
         offsets = const.tile([P, N // 16], U16, name="offsets")
         nc.sync.dma_start(offsets[:], offs)
@@ -60,7 +67,6 @@ def tile_lumiere1m_b_kernel(tc, emb, pe, wq, wk, wv, wo, ln_s, ln_b, offs, out):
         neg_half = const.tile([P, 1], F32, name="neg_half")
         nc.gpsimd.memset(neg_half[:], -0.5)
 
-        h_t = keep.tile([P, TB, C], F32, name="h_t")
         q_bf = keep.tile([P, H, N], BF16, name="q_bf")
         k_bf = keep.tile([P, H, N], BF16, name="k_bf")
         v_t = keep.tile([P, TB, C], BF16, name="v_t")
@@ -80,7 +86,7 @@ def tile_lumiere1m_b_kernel(tc, emb, pe, wq, wk, wv, wo, ln_s, ln_b, offs, out):
 
         with (
             tc.tile_pool(name="table", bufs=1) as table_pool,
-            tc.psum_pool(name="front_ps", bufs=2) as front_pool,
+            tc.psum_pool(name="front_ps", bufs=1) as front_pool,
         ):
             table = [table_pool.tile([P, S], F32, name=f"table{b}") for b in range(CB)]
             pe_sb = [table_pool.tile([P, N], F32, name=f"pe_sb{b}") for b in range(CB)]
@@ -109,19 +115,10 @@ def tile_lumiere1m_b_kernel(tc, emb, pe, wq, wk, wv, wo, ln_s, ln_b, offs, out):
                     )
                     nc.scalar.copy(h_bf[b][:, tokens], h[b][:, tokens])
 
-            def transpose_h(b):
-                for t0 in range(0, TB, 4):
-                    h_flip = flip_pool.tile([P, 4, P], F32, name="h_flip", tag="flip")
-                    for i in range(4):
-                        nc.tensor.transpose(
-                            h_flip[:, i, :], h[b][:, (t0 + i) * P : (t0 + i + 1) * P], ident_f32[:]
-                        )
-                    nc.scalar.copy(h_t[:, t0 : t0 + 4, b * P : (b + 1) * P], h_flip[:])
-
             def project(blocks_of, banks):
                 for n, (name, i) in enumerate(banks):
                     blocks = blocks_of[name]
-                    acc_pool = bank_pool if n % 3 < 2 else front_pool
+                    acc_pool = bank_pool if n % 5 < 4 else front_pool
                     acc = acc_pool.tile([P, BANK], F32, name="acc", tag="bank")
                     for b in blocks:
                         if name == "v":
@@ -142,24 +139,20 @@ def tile_lumiere1m_b_kernel(tc, emb, pe, wq, wk, wv, wo, ln_s, ln_b, offs, out):
                     else:
                         nc.vector.tensor_copy(partial[name][where], acc[:])
 
-            by_name = {name: [(name, i) for i in range(2 * H)] for name in ("q", "k", "v")}
+            by_name = {name: [(name, 2 * a + half) for half in range(2) for a in range(H)] for name in ("q", "k")}
+            by_name["v"] = [("v", i) for i in range(TB)]
             by_half = []
             for half in range(N // BANK):
-                for a in range(H):
-                    by_half.extend([("q", 2 * a + half), ("k", 2 * a + half)])
-                by_half.extend([("v", half * (TB // 2) + i) for i in range(TB // 2)])
+                by_half.append([(name, 2 * a + half) for a in range(H) for name in ("q", "k")])
+                by_half[half].extend([("v", half * (TB // 2) + i) for i in range(TB // 2)])
 
             look_up(0)
-            transpose_h(0)
             project(FIRST, by_name["q"])
             look_up(1)
-            transpose_h(1)
             project(FIRST, by_name["k"] + by_name["v"])
             for b in LATE:
                 look_up(b)
-            project(REST, by_half)
-            for b in LATE:
-                transpose_h(b)
+            project(REST, by_half[0])
 
         ln_ps = bank_pool.tile([P, P], F32, name="ln_ps", tag="bank")
         nc.tensor.transpose(ln_ps[:], ln_rows[:], ident_f32[:])
@@ -167,7 +160,7 @@ def tile_lumiere1m_b_kernel(tc, emb, pe, wq, wk, wv, wo, ln_s, ln_b, offs, out):
 
         with (
             tc.tile_pool(name="rows", bufs=6) as rows_pool,
-            tc.tile_pool(name="attn", bufs=2 * H + 2) as attn_pool,
+            tc.tile_pool(name="attn", bufs=2 * TURN) as attn_pool,
             tc.tile_pool(name="turned", bufs=4) as turned_pool,
             tc.tile_pool(name="small", bufs=8) as small,
             tc.tile_pool(name="tail", bufs=3) as tail,
@@ -176,7 +169,7 @@ def tile_lumiere1m_b_kernel(tc, emb, pe, wq, wk, wv, wo, ln_s, ln_b, offs, out):
 
             def exp_rows(t, a):
                 seen = (t + 1) * P
-                neg_sc = rows_pool.tile([P, N], F32, name="neg_sc")
+                neg_sc = rows_pool.tile([P, N], F32, name="neg_sc", tag="neg_sc")
                 neg_max = small.tile([P, 2], F32, name="neg_max")
                 pieces = range(0, seen, BANK)
                 for i, u0 in enumerate(pieces):
@@ -253,80 +246,102 @@ def tile_lumiere1m_b_kernel(tc, emb, pe, wq, wk, wv, wo, ln_s, ln_b, offs, out):
             def weigh(t, a, attn_t, o_ps):
                 for u in range(t + 1):
                     nc.tensor.matmul(
-                        o_ps[:, a, :],
+                        o_ps[:],
                         lhsT=v_t[:, u, a * DK : (a + 1) * DK],
                         rhs=attn_t[:, u * P : (u + 1) * P],
                         start=(u == 0),
                         stop=(u == t),
                     )
 
-            def normalised_residual(t, o_bf):
-                r_ps = one_pool.tile([P, C], F32, name="r_ps", tag="post")
+            def spare_bank(step, pool, tag, columns):
+                if step >= len(UNITS):
+                    pool, tag = bank_pool, "bank"
+                return pool.tile([P, columns], F32, name="spare", tag=tag)
+
+            def residual(t, o_bf, r_ps):
                 for a in range(H):
                     nc.tensor.matmul(
                         r_ps[:], lhsT=o_bf[:, a, :], rhs=wo_sb[:, a, :], start=(a == 0), stop=(a == H - 1)
                     )
-                r_t = tail.tile([P, C], F32, name="r_t")
-                nc.vector.tensor_tensor(r_t[:], r_ps[:], h_t[:, t, :], ALU.add)
+                    if a == 0:
+                        for b in range(CB):
+                            nc.tensor.matmul(
+                                r_ps[:, b * P : (b + 1) * P],
+                                lhsT=h[b][:, t * P : (t + 1) * P],
+                                rhs=ident_f32[:],
+                                is_transpose=True,
+                                start=False,
+                                stop=False,
+                            )
                 stats = small.tile([P, 6], F32, name="stats")
-                nc.vector.bn_stats(stats[:], r_t[:])
+                nc.vector.bn_stats(stats[:], r_ps[:])
                 mean_var = small.tile([P, 2], F32, name="mean_var")
                 nc.vector.bn_aggr(mean_var[:], stats[:])
                 var_eps = small.tile([P, 1], F32, name="var_eps")
                 nc.scalar.activation(out=var_eps[:], in_=mean_var[:, 1:2], func=FUNC.Copy, bias=EPS_LN)
-                neg_mean = small.tile([P, 1], F32, name="neg_mean")
-                nc.scalar.mul(neg_mean[:], mean_var[:, 0:1], -1.0)
                 inv_std = small.tile([P, 1], F32, name="inv_std")
                 nc.gpsimd.tensor_tensor(inv_std[:], var_eps[:], neg_half[:], ALU.pow)
-                y_t = tail.tile([P, C], F32, name="y_t")
-                nc.gpsimd.tensor_scalar(
-                    out=y_t[:], in0=r_t[:], scalar1=neg_mean[:], scalar2=inv_std[:], op0=ALU.add, op1=ALU.mult
+                return r_ps, mean_var, inv_std
+
+            def normalise_residual(r_ps, mean_var, inv_std):
+                y_t = rows_pool.tile([P, C], F32, name="y_t", tag="neg_sc")
+                nc.vector.tensor_scalar(
+                    out=y_t[:],
+                    in0=r_ps[:],
+                    scalar1=mean_var[:, 0:1],
+                    scalar2=inv_std[:],
+                    op0=ALU.subtract,
+                    op1=ALU.mult,
                 )
                 return y_t
 
-            def store(t, y_t):
-                y_ps = one_pool.tile([P, CB, P], F32, name="y_ps", tag="post")
+            def store(t, y_t, y_ps):
                 for b in range(CB):
-                    nc.tensor.transpose(y_ps[:, b, :], y_t[:, b * P : (b + 1) * P], ident_f32[:])
+                    nc.tensor.transpose(y_ps[:, b * P : (b + 1) * P], y_t[:, b * P : (b + 1) * P], ident_f32[:])
                 out_sb = tail.tile([P, CB, P], F32, name="out_sb")
                 for b in range(CB):
                     nc.scalar.activation(
                         out=out_sb[:, b, :],
-                        in_=y_ps[:, b, :],
+                        in_=y_ps[:, b * P : (b + 1) * P],
                         func=FUNC.Identity,
                         bias=ln_cols[:, CB + b : CB + b + 1],
                         scale=ln_cols[:, b : b + 1],
                     )
                 nc.sync.dma_start(out_blocks[:, :, t * P : (t + 1) * P], out_sb[:])
 
+            exps = {}
             attn_of = {}
+            turned_of = {}
             o_of = {}
+            r_of = {}
             y_of = {}
-            for step in range(TB + 3):
-                first = BLOCKS[step] if step < TB else None
-                second = BLOCKS[step - 1] if 1 <= step <= TB else None
-                third = BLOCKS[step - 2] if 2 <= step <= TB + 1 else None
-                fourth = BLOCKS[step - 3] if step >= 3 else None
-                if first is not None:
-                    attn_of[first] = []
-                if second is not None:
-                    o_ps = one_pool.tile([P, H, P], F32, name="o_ps")
-                    o_of[second] = tail.tile([P, H, P], BF16, name="o_bf")
-                for a in range(H + 1):
-                    if first is not None and a < H:
-                        exps = exp_rows(first, a)
-                    if first is not None and a > 0:
-                        attn_of[first].append(normalise(first, *waiting_exps))
-                    if second is not None and a < H:
-                        turned = turn(second, a, attn_of[second][a])
-                    if second is not None and a > 0:
-                        weigh(second, a - 1, waiting_turned, o_ps)
-                        nc.scalar.copy(o_of[second][:, a - 1, :], o_ps[:, a - 1, :])
-                    if first is not None:
-                        waiting_exps = exps
-                    if second is not None:
-                        waiting_turned = turned
-                if third is not None:
-                    y_of[third] = normalised_residual(third, o_of[third])
-                if fourth is not None:
-                    store(fourth, y_of[fourth])
+            for step in range(len(UNITS) + STORE):
+                unit = {lag: step - lag for lag in (0, NORMALISE, TURN, WEIGH, RESIDUAL, CENTRE, STORE)}
+                unit = {lag: n for lag, n in unit.items() if 0 <= n < len(UNITS)}
+                late = step - LATE_FROM
+                if 0 <= late < len(by_half[1]):
+                    project(REST, by_half[1][late : late + 1])
+                if 0 in unit:
+                    exps[step] = exp_rows(*UNITS[step])
+                if NORMALISE in unit:
+                    n = unit[NORMALISE]
+                    attn_of[n] = normalise(UNITS[n][0], *exps[n])
+                if TURN in unit:
+                    n = unit[TURN]
+                    turned_of[n] = turn(*UNITS[n], attn_of[n])
+                if WEIGH in unit:
+                    t, a = UNITS[unit[WEIGH]]
+                    if a == 0:
+                        o_of[t] = tail.tile([P, H, P], BF16, name="o_bf")
+                    o_ps = spare_bank(step, flip_pool, "flip", P)
+                    weigh(t, a, turned_of[unit[WEIGH]], o_ps)
+                    nc.scalar.copy(o_of[t][:, a, :], o_ps[:])
+                if RESIDUAL in unit and UNITS[unit[RESIDUAL]][1] == H - 1:
+                    t = UNITS[unit[RESIDUAL]][0]
+                    r_of[t] = residual(t, o_of[t], spare_bank(step, one_pool, "post", C))
+                if CENTRE in unit and UNITS[unit[CENTRE]][1] == H - 1:
+                    t = UNITS[unit[CENTRE]][0]
+                    y_of[t] = normalise_residual(*r_of[t])
+                if STORE in unit and UNITS[unit[STORE]][1] == H - 1:
+                    t = UNITS[unit[STORE]][0]
+                    store(t, y_of[t], spare_bank(step, flip_pool, "flip", C))

@@ -229,12 +229,8 @@ def tile_lumiere1m_b_kernel(tc, emb, pe, wq, wk, wv, wo, ln_s, ln_b, offs, out):
                 seen = (t + 1) * P
                 attn_flip = flip_pool.tile([P, N], BF16, name="attn_flip", tag="flip")
                 for u in range(t + 1):
-                    nc.tensor.matmul(
-                        attn_flip[:, u * P : (u + 1) * P],
-                        lhsT=attn[:, u * P : (u + 1) * P],
-                        rhs=ident_bf[:],
-                        start=True,
-                        stop=True,
+                    nc.tensor.transpose(
+                        attn_flip[:, u * P : (u + 1) * P], attn[:, u * P : (u + 1) * P], ident_bf[:]
                     )
                 attn_t = turned_pool.tile([P, N], BF16, name="attn_t")
                 if a % 2 == 0:

@@ -22,6 +22,7 @@ BANK = 512
 SCALE = 1.0 / math.sqrt(DK)
 EPS_SM = 1e-9
 EPS_LN = 1e-5
+SUMS = 8
 MASKED = -1e30
 EARLY = (0, 1)
 LATE = (2, 3)
@@ -48,8 +49,8 @@ def tile_lumiere1m_b_kernel(tc, emb, pe, wq, wk, wv, wo, ln_s, ln_b, offs, out):
     with (
         tc.tile_pool(name="const", bufs=1) as const,
         tc.tile_pool(name="keep", bufs=1) as keep,
-        tc.psum_pool(name="bank_ps", bufs=4) as bank_pool,
-        tc.psum_pool(name="flip_ps", bufs=3) as flip_pool,
+        tc.psum_pool(name="bank_ps", bufs=7) as bank_pool,
+        tc.psum_pool(name="post_ps", bufs=1) as post_pool,
     ):
         offsets = const.tile([P, N // 16], U16, name="offsets")
         nc.sync.dma_start(offsets[:], offs)
@@ -64,6 +65,8 @@ def tile_lumiere1m_b_kernel(tc, emb, pe, wq, wk, wv, wo, ln_s, ln_b, offs, out):
         nc.vector.tensor_scalar(
             out=causal[:], in0=ahead[:], scalar1=0.0, scalar2=MASKED, op0=ALU.is_ge, op1=ALU.mult
         )
+        sums = const.tile([P, SUMS, 2], F32, name="sums")
+        nc.vector.memset(sums[:], EPS_SM)
         neg_half = const.tile([P, 1], F32, name="neg_half")
         nc.gpsimd.memset(neg_half[:], -0.5)
 
@@ -86,7 +89,6 @@ def tile_lumiere1m_b_kernel(tc, emb, pe, wq, wk, wv, wo, ln_s, ln_b, offs, out):
 
         with (
             tc.tile_pool(name="table", bufs=1) as table_pool,
-            tc.psum_pool(name="front_ps", bufs=1) as front_pool,
         ):
             table = [table_pool.tile([P, S], F32, name=f"table{b}") for b in range(CB)]
             pe_sb = [table_pool.tile([P, N], F32, name=f"pe_sb{b}") for b in range(CB)]
@@ -118,8 +120,7 @@ def tile_lumiere1m_b_kernel(tc, emb, pe, wq, wk, wv, wo, ln_s, ln_b, offs, out):
             def project(blocks_of, banks):
                 for n, (name, i) in enumerate(banks):
                     blocks = blocks_of[name]
-                    acc_pool = bank_pool if n % 5 < 4 else front_pool
-                    acc = acc_pool.tile([P, BANK], F32, name="acc", tag="bank")
+                    acc = bank_pool.tile([P, BANK], F32, name="acc", tag="bank")
                     for b in blocks:
                         if name == "v":
                             lhs_t, rhs = h_bf[b][:, i * P : (i + 1) * P], w_sb["v"][:, b, :]
@@ -164,10 +165,10 @@ def tile_lumiere1m_b_kernel(tc, emb, pe, wq, wk, wv, wo, ln_s, ln_b, offs, out):
             tc.tile_pool(name="turned", bufs=4) as turned_pool,
             tc.tile_pool(name="small", bufs=8) as small,
             tc.tile_pool(name="tail", bufs=3) as tail,
-            tc.psum_pool(name="one_ps", bufs=1) as one_pool,
         ):
 
             def exp_rows(t, a):
+                total = sums[:, (t * H + a) % SUMS, :]
                 seen = (t + 1) * P
                 neg_sc = rows_pool.tile([P, N], F32, name="neg_sc", tag="neg_sc")
                 neg_max = small.tile([P, 2], F32, name="neg_max")
@@ -197,21 +198,20 @@ def tile_lumiere1m_b_kernel(tc, emb, pe, wq, wk, wv, wo, ln_s, ln_b, offs, out):
                         accum_out=neg_max[:, i : i + 1],
                     )
                 e = rows_pool.tile([P, N], F32, name="e")
-                total = small.tile([P, 1], F32, name="total")
                 nc.scalar.activation(
                     out=e[:, :seen],
                     in_=neg_sc[:, :seen],
                     func=FUNC.Exp,
                     bias=neg_max[:, len(pieces) - 1 : len(pieces)],
                     scale=-1.0,
-                    accum_out=total[:],
+                    accum_out=total[:, 0:1],
                 )
-                padded = small.tile([P, 1], F32, name="padded")
-                nc.scalar.activation(out=padded[:], in_=total[:], func=FUNC.Copy, bias=EPS_SM)
-                return e, padded
+                return e, total
 
-            def normalise(t, e, padded):
+            def normalise(t, e, total):
                 seen = (t + 1) * P
+                padded = small.tile([P, 1], F32, name="padded")
+                nc.vector.tensor_reduce(padded[:], total, mybir.AxisListType.X, ALU.add)
                 inv_total = small.tile([P, 1], F32, name="inv_total")
                 nc.vector.reciprocal(inv_total[:], padded[:])
                 attn = attn_pool.tile([P, N], BF16, name="attn")
@@ -227,7 +227,7 @@ def tile_lumiere1m_b_kernel(tc, emb, pe, wq, wk, wv, wo, ln_s, ln_b, offs, out):
 
             def turn(t, a, attn):
                 seen = (t + 1) * P
-                attn_flip = flip_pool.tile([P, N], BF16, name="attn_flip", tag="flip")
+                attn_flip = bank_pool.tile([P, N], BF16, name="attn_flip", tag="bank")
                 for u in range(t + 1):
                     nc.tensor.transpose(
                         attn_flip[:, u * P : (u + 1) * P], attn[:, u * P : (u + 1) * P], ident_bf[:]
@@ -249,10 +249,10 @@ def tile_lumiere1m_b_kernel(tc, emb, pe, wq, wk, wv, wo, ln_s, ln_b, offs, out):
                         stop=(u == t),
                     )
 
-            def spare_bank(step, pool, tag, columns):
-                if step >= len(UNITS):
-                    pool, tag = bank_pool, "bank"
-                return pool.tile([P, columns], F32, name="spare", tag=tag)
+            def residual_bank(step):
+                if step < len(UNITS):
+                    return post_pool.tile([P, C], F32, name="r_ps", tag="post")
+                return bank_pool.tile([P, C], F32, name="r_ps", tag="bank")
 
             def residual(t, o_bf, r_ps):
                 for a in range(H):
@@ -329,15 +329,15 @@ def tile_lumiere1m_b_kernel(tc, emb, pe, wq, wk, wv, wo, ln_s, ln_b, offs, out):
                     t, a = UNITS[unit[WEIGH]]
                     if a == 0:
                         o_of[t] = tail.tile([P, H, P], BF16, name="o_bf")
-                    o_ps = spare_bank(step, flip_pool, "flip", P)
+                    o_ps = bank_pool.tile([P, P], F32, name="o_ps", tag="bank")
                     weigh(t, a, turned_of[unit[WEIGH]], o_ps)
                     nc.scalar.copy(o_of[t][:, a, :], o_ps[:])
                 if RESIDUAL in unit and UNITS[unit[RESIDUAL]][1] == H - 1:
                     t = UNITS[unit[RESIDUAL]][0]
-                    r_of[t] = residual(t, o_of[t], spare_bank(step, one_pool, "post", C))
+                    r_of[t] = residual(t, o_of[t], residual_bank(step))
                 if CENTRE in unit and UNITS[unit[CENTRE]][1] == H - 1:
                     t = UNITS[unit[CENTRE]][0]
                     y_of[t] = normalise_residual(*r_of[t])
                 if STORE in unit and UNITS[unit[STORE]][1] == H - 1:
                     t = UNITS[unit[STORE]][0]
-                    store(t, y_of[t], spare_bank(step, flip_pool, "flip", C))
+                    store(t, y_of[t], bank_pool.tile([P, C], F32, name="y_ps", tag="bank"))

@@ -29,7 +29,8 @@ LATE = (2, 3)
 FIRST = {"q": (0,), "k": (0, 1), "v": (0, 1)}
 REST = {"q": (1, 2, 3), "k": (2, 3), "v": (2, 3)}
 UNITS = [(t, a) for t in range(TB) for a in range(H)]
-NORMALISE = 1
+PAD = 1
+NORMALISE = 2
 TURN = 6
 WEIGH = 8
 RESIDUAL = 9
@@ -160,10 +161,10 @@ def tile_lumiere1m_b_kernel(tc, emb, pe, wq, wk, wv, wo, ln_s, ln_b, offs, out):
         nc.vector.tensor_copy(ln_cols[:], ln_ps[:, 0 : 2 * CB])
 
         with (
-            tc.tile_pool(name="rows", bufs=6) as rows_pool,
+            tc.tile_pool(name="rows", bufs=7) as rows_pool,
             tc.tile_pool(name="attn", bufs=2 * TURN) as attn_pool,
             tc.tile_pool(name="turned", bufs=4) as turned_pool,
-            tc.tile_pool(name="small", bufs=8) as small,
+            tc.tile_pool(name="small", bufs=16) as small,
             tc.tile_pool(name="tail", bufs=3) as tail,
         ):
 
@@ -208,11 +209,14 @@ def tile_lumiere1m_b_kernel(tc, emb, pe, wq, wk, wv, wo, ln_s, ln_b, offs, out):
                 )
                 return e, total
 
-            def normalise(t, e, total):
-                seen = (t + 1) * P
-                padded = small.tile([P, 1], F32, name="padded")
+            def pad(total):
+                padded = small.tile([P, 1], F32, name="padded", tag="neg_max")
                 nc.vector.tensor_reduce(padded[:], total, mybir.AxisListType.X, ALU.add)
-                inv_total = small.tile([P, 1], F32, name="inv_total")
+                return padded
+
+            def normalise(t, e, padded):
+                seen = (t + 1) * P
+                inv_total = small.tile([P, 1], F32, name="inv_total", tag="neg_max")
                 nc.vector.reciprocal(inv_total[:], padded[:])
                 attn = attn_pool.tile([P, N], BF16, name="attn")
                 nc.gpsimd.tensor_scalar(
@@ -306,22 +310,26 @@ def tile_lumiere1m_b_kernel(tc, emb, pe, wq, wk, wv, wo, ln_s, ln_b, offs, out):
                 nc.sync.dma_start(out_blocks[:, :, t * P : (t + 1) * P], out_sb[:])
 
             exps = {}
+            padded_of = {}
             attn_of = {}
             turned_of = {}
             o_of = {}
             r_of = {}
             y_of = {}
             for step in range(len(UNITS) + STORE):
-                unit = {lag: step - lag for lag in (0, NORMALISE, TURN, WEIGH, RESIDUAL, CENTRE, STORE)}
+                unit = {lag: step - lag for lag in (0, PAD, NORMALISE, TURN, WEIGH, RESIDUAL, CENTRE, STORE)}
                 unit = {lag: n for lag, n in unit.items() if 0 <= n < len(UNITS)}
                 late = step - LATE_FROM
                 if 0 <= late < len(by_half[1]):
                     project(REST, by_half[1][late : late + 1])
                 if 0 in unit:
                     exps[step] = exp_rows(*UNITS[step])
+                if PAD in unit:
+                    n = unit[PAD]
+                    padded_of[n] = pad(exps[n][1])
                 if NORMALISE in unit:
                     n = unit[NORMALISE]
-                    attn_of[n] = normalise(UNITS[n][0], *exps[n])
+                    attn_of[n] = normalise(UNITS[n][0], exps[n][0], padded_of[n])
                 if TURN in unit:
                     n = unit[TURN]
                     turned_of[n] = turn(*UNITS[n], attn_of[n])

@@ -34,9 +34,9 @@ NORMALISE = 2
 TURN = 6
 WEIGH = 8
 RESIDUAL = 9
-CENTRE = 12
+CENTRE = 13
 LATE_FROM = 2
-STORE = 15
+STORE = 16
 
 FLOPS = 2 * C * C * N * 4 + 2 * 2 * H * DK * (N * (N - 1) // 2)
 

import math

import concourse.mybir as mybir
from concourse.masks import make_identity

F32 = mybir.dt.float32
BF16 = mybir.dt.bfloat16
U16 = mybir.dt.uint16
I32 = mybir.dt.int32
ALU = mybir.AluOpType
FUNC = mybir.ActivationFunctionType

P = 128
C = 512
S = 4096
N = 1024
H = 4
DK = 128
CB = C // P
TB = N // P
BANK = 512
SCALE = 1.0 / math.sqrt(DK)
EPS_SM = 1e-9
EPS_LN = 1e-5
SUMS = 8
MASKED = -1e30
EARLY = (0, 1)
LATE = (2, 3)
FIRST = {"q": (0,), "k": (0, 1), "v": (0, 1)}
REST = {"q": (1, 2, 3), "k": (2, 3), "v": (2, 3)}
UNITS = [(t, a) for t in range(TB) for a in range(H)]
PAD = 1
NORMALISE = 2
TURN = 6
WEIGH = 8
RESIDUAL = 9
CENTRE = 13
LATE_FROM = 2
STORE = 16

FLOPS = 2 * C * C * N * 4 + 2 * 2 * H * DK * (N * (N - 1) // 2)


def tile_lumiere1m_b_kernel(tc, emb, pe, wq, wk, wv, wo, ln_s, ln_b, offs, out):
    nc = tc.nc
    emb_blocks = emb.rearrange("(b p) s -> b p s", p=P)
    pe_blocks = pe.rearrange("(b p) n -> b p n", p=P)
    out_blocks = out.rearrange("(b p) n -> p b n", p=P)

    with (
        tc.tile_pool(name="const", bufs=1) as const,
        tc.tile_pool(name="keep", bufs=1) as keep,
        tc.psum_pool(name="bank_ps", bufs=7) as bank_pool,
        tc.psum_pool(name="post_ps", bufs=1) as post_pool,
    ):
        offsets = const.tile([P, N // 16], U16, name="offsets")
        nc.sync.dma_start(offsets[:], offs)

        ident_f32 = const.tile([P, P], F32, name="ident_f32")
        make_identity(nc, ident_f32[:])
        ident_bf = const.tile([P, P], BF16, name="ident_bf")
        make_identity(nc, ident_bf[:])
        ahead = const.tile([P, P], I32, name="ahead")
        nc.gpsimd.iota(ahead[:], pattern=[[1, P]], base=0, channel_multiplier=-1)
        causal = const.tile([P, P], BF16, name="causal")
        nc.vector.tensor_scalar(
            out=causal[:], in0=ahead[:], scalar1=0.0, scalar2=MASKED, op0=ALU.is_ge, op1=ALU.mult
        )
        sums = const.tile([P, SUMS, 2], F32, name="sums")
        nc.vector.memset(sums[:], EPS_SM)
        neg_half = const.tile([P, 1], F32, name="neg_half")
        nc.gpsimd.memset(neg_half[:], -0.5)

        q_bf = keep.tile([P, H, N], BF16, name="q_bf")
        k_bf = keep.tile([P, H, N], BF16, name="k_bf")
        v_t = keep.tile([P, TB, C], BF16, name="v_t")
        projected = {"q": q_bf, "k": k_bf, "v": v_t}
        partial = {
            "q": keep.tile([P, H, N], F32, name="q_part"),
            "k": keep.tile([P, H, N], F32, name="k_part"),
            "v": keep.tile([P, TB, C], F32, name="v_part"),
        }
        w_sb = {name: keep.tile([P, CB, C], BF16, name=f"w{name}_sb") for name in ("q", "k", "v")}
        wo_sb = keep.tile([P, H, C], BF16, name="wo_sb")
        ln_rows = keep.tile([P, P], F32, name="ln_rows")
        ln_cols = keep.tile([P, 2 * CB], F32, name="ln_cols")
        h = [keep.tile([P, N], F32, name=f"h{b}") for b in range(CB)]
        h_bf = [keep.tile([P, N], BF16, name=f"h_bf{b}") for b in range(CB)]
        nc.gpsimd.memset(ln_rows[:], 0.0)

        with (
            tc.tile_pool(name="table", bufs=1) as table_pool,
        ):
            table = [table_pool.tile([P, S], F32, name=f"table{b}") for b in range(CB)]
            pe_sb = [table_pool.tile([P, N], F32, name=f"pe_sb{b}") for b in range(CB)]
            def load_weights(name, w, blocks):
                rows = w.rearrange("(b p) m -> p b m", p=P)
                nc.sync.dma_start(w_sb[name][:, blocks[0] : blocks[-1] + 1, :], rows[:, blocks[0] : blocks[-1] + 1, :])

            for blocks in (EARLY, LATE):
                for b in blocks:
                    nc.sync.dma_start(table[b][:], emb_blocks[b])
                    nc.sync.dma_start(pe_sb[b][:], pe_blocks[b])
                    if b == blocks[0]:
                        load_weights("q", wq, blocks)
                load_weights("k", wk, blocks)
                load_weights("v", wv, blocks)
            nc.sync.dma_start(wo_sb[:], wo.rearrange("(a p) c -> p a c", p=P))
            nc.sync.dma_start(ln_rows[0:CB, :], ln_s.rearrange("(b p) o -> b (p o)", p=P))
            nc.sync.dma_start(ln_rows[CB : 2 * CB, :], ln_b.rearrange("(b p) o -> b (p o)", p=P))

            def look_up(b):
                for half in range(N // BANK):
                    tokens = slice(half * BANK, (half + 1) * BANK)
                    piece = offsets[:, half * (BANK // 16) : (half + 1) * (BANK // 16)]
                    nc.vector.tensor_tensor(
                        h[b][:, tokens], table[b][:].indirect(piece), pe_sb[b][:, tokens], ALU.add
                    )
                    nc.scalar.copy(h_bf[b][:, tokens], h[b][:, tokens])

            def project(blocks_of, banks):
                for n, (name, i) in enumerate(banks):
                    blocks = blocks_of[name]
                    acc = bank_pool.tile([P, BANK], F32, name="acc", tag="bank")
                    for b in blocks:
                        if name == "v":
                            lhs_t, rhs = h_bf[b][:, i * P : (i + 1) * P], w_sb["v"][:, b, :]
                        else:
                            a, half = i // 2, i % 2
                            lhs_t = w_sb[name][:, b, a * DK : (a + 1) * DK]
                            rhs = h_bf[b][:, half * BANK : (half + 1) * BANK]
                        nc.tensor.matmul(acc[:], lhsT=lhs_t, rhs=rhs, start=(b == blocks[0]), stop=(b == blocks[-1]))
                    if name == "v":
                        where = (slice(None), i, slice(None))
                    else:
                        where = (slice(None), i // 2, slice((i % 2) * BANK, (i % 2 + 1) * BANK))
                    if blocks_of == REST:
                        nc.vector.tensor_tensor(projected[name][where], acc[:], partial[name][where], ALU.add)
                    elif n % 2 == 0:
                        nc.scalar.copy(partial[name][where], acc[:])
                    else:
                        nc.vector.tensor_copy(partial[name][where], acc[:])

            by_name = {name: [(name, 2 * a + half) for half in range(2) for a in range(H)] for name in ("q", "k")}
            by_name["v"] = [("v", i) for i in range(TB)]
            by_half = []
            for half in range(N // BANK):
                by_half.append([(name, 2 * a + half) for a in range(H) for name in ("q", "k")])
                by_half[half].extend([("v", half * (TB // 2) + i) for i in range(TB // 2)])

            look_up(0)
            project(FIRST, by_name["q"])
            look_up(1)
            project(FIRST, by_name["k"] + by_name["v"])
            for b in LATE:
                look_up(b)
            project(REST, by_half[0])

        ln_ps = bank_pool.tile([P, P], F32, name="ln_ps", tag="bank")
        nc.tensor.transpose(ln_ps[:], ln_rows[:], ident_f32[:])
        nc.vector.tensor_copy(ln_cols[:], ln_ps[:, 0 : 2 * CB])

        with (
            tc.tile_pool(name="rows", bufs=7) as rows_pool,
            tc.tile_pool(name="attn", bufs=2 * TURN) as attn_pool,
            tc.tile_pool(name="turned", bufs=4) as turned_pool,
            tc.tile_pool(name="small", bufs=16) as small,
            tc.tile_pool(name="tail", bufs=3) as tail,
        ):

            def exp_rows(t, a):
                total = sums[:, (t * H + a) % SUMS, :]
                seen = (t + 1) * P
                neg_sc = rows_pool.tile([P, N], F32, name="neg_sc", tag="neg_sc")
                neg_max = small.tile([P, 2], F32, name="neg_max")
                pieces = range(0, seen, BANK)
                for i, u0 in enumerate(pieces):
                    width = min(BANK, seen - u0)
                    sc = bank_pool.tile([P, BANK], F32, name="sc", tag="bank")
                    last = u0 + width == seen
                    nc.tensor.matmul(
                        sc[:, :width],
                        lhsT=q_bf[:, a, t * P : (t + 1) * P],
                        rhs=k_bf[:, a, u0 : u0 + width],
                        start=True,
                        stop=not last,
                    )
                    if last:
                        nc.tensor.matmul(
                            sc[:, width - P : width], lhsT=ident_bf[:], rhs=causal[:], start=False, stop=True
                        )
                    nc.vector.tensor_scalar(
                        out=neg_sc[:, u0 : u0 + width],
                        in0=sc[:, :width],
                        scalar1=-SCALE,
                        scalar2=0.0 if i == 0 else neg_max[:, i - 1 : i],
                        op0=ALU.mult,
                        op1=ALU.min,
                        accum_out=neg_max[:, i : i + 1],
                    )
                e = rows_pool.tile([P, N], F32, name="e")
                nc.scalar.activation(
                    out=e[:, :seen],
                    in_=neg_sc[:, :seen],
                    func=FUNC.Exp,
                    bias=neg_max[:, len(pieces) - 1 : len(pieces)],
                    scale=-1.0,
                    accum_out=total[:, 0:1],
                )
                return e, total

            def pad(total):
                padded = small.tile([P, 1], F32, name="padded", tag="neg_max")
                nc.vector.tensor_reduce(padded[:], total, mybir.AxisListType.X, ALU.add)
                return padded

            def normalise(t, e, padded):
                seen = (t + 1) * P
                inv_total = small.tile([P, 1], F32, name="inv_total", tag="neg_max")
                nc.vector.reciprocal(inv_total[:], padded[:])
                attn = attn_pool.tile([P, N], BF16, name="attn")
                nc.gpsimd.tensor_scalar(
                    out=attn[:, :seen],
                    in0=e[:, :seen],
                    scalar1=inv_total[:],
                    scalar2=0.0,
                    op0=ALU.mult,
                    op1=ALU.add,
                )
                return attn

            def turn(t, a, attn):
                seen = (t + 1) * P
                attn_flip = bank_pool.tile([P, N], BF16, name="attn_flip", tag="bank")
                for u in range(t + 1):
                    nc.tensor.transpose(
                        attn_flip[:, u * P : (u + 1) * P], attn[:, u * P : (u + 1) * P], ident_bf[:]
                    )
                attn_t = turned_pool.tile([P, N], BF16, name="attn_t")
                if a % 2 == 0:
                    nc.vector.tensor_copy(attn_t[:, :seen], attn_flip[:, :seen])
                else:
                    nc.scalar.copy(attn_t[:, :seen], attn_flip[:, :seen])
                return attn_t

            def weigh(t, a, attn_t, o_ps):
                for u in range(t + 1):
                    nc.tensor.matmul(
                        o_ps[:],
                        lhsT=v_t[:, u, a * DK : (a + 1) * DK],
                        rhs=attn_t[:, u * P : (u + 1) * P],
                        start=(u == 0),
                        stop=(u == t),
                    )

            def residual_bank(step):
                if step < len(UNITS):
                    return post_pool.tile([P, C], F32, name="r_ps", tag="post")
                return bank_pool.tile([P, C], F32, name="r_ps", tag="bank")

            def residual(t, o_bf, r_ps):
                for a in range(H):
                    nc.tensor.matmul(
                        r_ps[:], lhsT=o_bf[:, a, :], rhs=wo_sb[:, a, :], start=(a == 0), stop=(a == H - 1)
                    )
                    if a == 0:
                        for b in range(CB):
                            nc.tensor.matmul(
                                r_ps[:, b * P : (b + 1) * P],
                                lhsT=h[b][:, t * P : (t + 1) * P],
                                rhs=ident_f32[:],
                                is_transpose=True,
                                start=False,
                                stop=False,
                            )
                stats = small.tile([P, 6], F32, name="stats")
                nc.vector.bn_stats(stats[:], r_ps[:])
                mean_var = small.tile([P, 2], F32, name="mean_var")
                nc.vector.bn_aggr(mean_var[:], stats[:])
                var_eps = small.tile([P, 1], F32, name="var_eps")
                nc.scalar.activation(out=var_eps[:], in_=mean_var[:, 1:2], func=FUNC.Copy, bias=EPS_LN)
                inv_std = small.tile([P, 1], F32, name="inv_std")
                nc.gpsimd.tensor_tensor(inv_std[:], var_eps[:], neg_half[:], ALU.pow)
                return r_ps, mean_var, inv_std

            def normalise_residual(r_ps, mean_var, inv_std):
                y_t = rows_pool.tile([P, C], F32, name="y_t", tag="neg_sc")
                nc.vector.tensor_scalar(
                    out=y_t[:],
                    in0=r_ps[:],
                    scalar1=mean_var[:, 0:1],
                    scalar2=inv_std[:],
                    op0=ALU.subtract,
                    op1=ALU.mult,
                )
                return y_t

            def store(t, y_t, y_ps):
                for b in range(CB):
                    nc.tensor.transpose(y_ps[:, b * P : (b + 1) * P], y_t[:, b * P : (b + 1) * P], ident_f32[:])
                out_sb = tail.tile([P, CB, P], F32, name="out_sb")
                for b in range(CB):
                    nc.scalar.activation(
                        out=out_sb[:, b, :],
                        in_=y_ps[:, b * P : (b + 1) * P],
                        func=FUNC.Identity,
                        bias=ln_cols[:, CB + b : CB + b + 1],
                        scale=ln_cols[:, b : b + 1],
                    )
                nc.sync.dma_start(out_blocks[:, :, t * P : (t + 1) * P], out_sb[:])

            exps = {}
            padded_of = {}
            attn_of = {}
            turned_of = {}
            o_of = {}
            r_of = {}
            y_of = {}
            for step in range(len(UNITS) + STORE):
                unit = {lag: step - lag for lag in (0, PAD, NORMALISE, TURN, WEIGH, RESIDUAL, CENTRE, STORE)}
                unit = {lag: n for lag, n in unit.items() if 0 <= n < len(UNITS)}
                late = step - LATE_FROM
                if 0 <= late < len(by_half[1]):
                    project(REST, by_half[1][late : late + 1])
                if 0 in unit:
                    exps[step] = exp_rows(*UNITS[step])
                if PAD in unit:
                    n = unit[PAD]
                    padded_of[n] = pad(exps[n][1])
                if NORMALISE in unit:
                    n = unit[NORMALISE]
                    attn_of[n] = normalise(UNITS[n][0], exps[n][0], padded_of[n])
                if TURN in unit:
                    n = unit[TURN]
                    turned_of[n] = turn(*UNITS[n], attn_of[n])
                if WEIGH in unit:
                    t, a = UNITS[unit[WEIGH]]
                    if a == 0:
                        o_of[t] = tail.tile([P, H, P], BF16, name="o_bf")
                    o_ps = bank_pool.tile([P, P], F32, name="o_ps", tag="bank")
                    weigh(t, a, turned_of[unit[WEIGH]], o_ps)
                    nc.scalar.copy(o_of[t][:, a, :], o_ps[:])
                if RESIDUAL in unit and UNITS[unit[RESIDUAL]][1] == H - 1:
                    t = UNITS[unit[RESIDUAL]][0]
                    r_of[t] = residual(t, o_of[t], residual_bank(step))
                if CENTRE in unit and UNITS[unit[CENTRE]][1] == H - 1:
                    t = UNITS[unit[CENTRE]][0]
                    y_of[t] = normalise_residual(*r_of[t])
                if STORE in unit and UNITS[unit[STORE]][1] == H - 1:
                    t = UNITS[unit[STORE]][0]
                    store(t, y_of[t], bank_pool.tile([P, C], F32, name="y_ps", tag="bank"))
